import numpy as np
import ml_dtypes


def mxq(x, axis, fmt="e4m3"):
    dtype, down = {"e4m3": (ml_dtypes.float8_e4m3fn, 7), "e5m2": (ml_dtypes.float8_e5m2, 14)}[fmt]
    v = np.moveaxis(np.asarray(x, np.float32).astype(ml_dtypes.bfloat16).astype(np.float64), axis, -1)
    blocks = v.reshape(v.shape[:-1] + (-1, 32))
    amax = np.abs(blocks).max(-1, keepdims=True)
    byte = np.maximum(np.where(amax > 0, np.frexp(amax)[1] - 1 + 127, 0) - down, 1)
    scale = np.exp2(byte - 127.0)
    codes = (blocks / scale).astype(np.float32).astype(dtype).astype(np.float64)
    return np.moveaxis((codes * scale).reshape(v.shape), -1, axis)


WIDE = False


def mx_kscale(k):
    if not WIDE:
        return np.ones(k)
    levels = np.array([10, -10, 5, -5, 0])
    a = np.random.permutation(np.resize(levels, k // 512 * 4)).reshape(k // 512, 4)
    idx = np.arange(k)
    return np.exp2(a[idx // 512, idx % 128 // 32])


BF16 = ml_dtypes.bfloat16


def bf(x):
    return np.asarray(x, np.float32).astype(BF16)


def f64(x):
    return np.asarray(x).astype(np.float64)


B, S, DIM, H, HD = 4, 128, 2048, 16, 128
E = H * HD


def rope_tables():
    inv_freq = 1.0 / (10000.0 ** (np.arange(0, HD, 2) / HD))
    freqs = np.outer(np.arange(S), inv_freq)
    emb = np.concatenate([freqs, freqs], axis=-1)
    return np.cos(emb)[None, None], np.sin(emb)[None, None]


def rotate_half(x):
    x1, x2 = np.split(x, 2, axis=-1)
    return np.concatenate([-x2, x1], axis=-1)


def setup_inputs():
    s = mx_kscale(DIM)
    cos, sin = rope_tables()
    return {"key_value": bf(np.random.standard_normal((B, S, DIM)) * s),
            "wk": bf(np.random.standard_normal((E, DIM)) / np.sqrt(DIM) / s),
            "bk": bf(np.random.standard_normal(E) * 0.1),
            "wv": bf(np.random.standard_normal((E, DIM)) / np.sqrt(DIM) / s),
            "bv": bf(np.random.standard_normal(E) * 0.1),
            "cos": bf(cos), "sin": bf(sin)}


def reference(key_value, wk, bk, wv, bv, cos, sin):
    xq = mxq(f64(key_value), 2, "e4m3")
    k = (xq @ mxq(f64(wk), 1, "e4m3").T) + f64(bk)
    v = (xq @ mxq(f64(wv), 1, "e4m3").T) + f64(bv)
    k = k.reshape(B, S, H, HD).transpose(0, 2, 1, 3)
    v = v.reshape(B, S, H, HD).transpose(0, 2, 1, 3)
    k = k * f64(cos) + rotate_half(k) * f64(sin)
    return k, v

@@ -1,0 +1,297 @@
+from contextlib import ExitStack
+
+import concourse.mybir as mybir
+from concourse.masks import make_identity
+
+F32 = mybir.dt.float32
+BF16 = mybir.dt.bfloat16
+U32 = mybir.dt.uint32
+U8 = mybir.dt.uint8
+I32 = mybir.dt.int32
+FP8X4 = mybir.dt.float8_e4m3fn_x4
+ADD = mybir.AluOpType.add
+MULT = mybir.AluOpType.mult
+
+P = 128
+B, S, DIM, H, HD = 4, 128, 2048, 16, 128
+FLOPS = 2 * B * S * DIM * 2 * H * HD
+
+SIN_ON_GPSIMD = False
+DEFER_A = 2
+DEFER_B = 1
+CHUNKS = [(True, 0), (False, 0), (True, 1), (False, 1), (True, 2), (False, 2), (True, 3), (False, 3)]
+LAST = len(CHUNKS) - 1
+
+
+def tile_attention_pb_kernel(tc, key_value, wk, bk, wv, bv, cos, sin, out_0, out_1):
+    nc = tc.nc
+    with ExitStack() as ctx:
+        const = ctx.enter_context(tc.tile_pool(name="const", bufs=1))
+        rawp = ctx.enter_context(tc.tile_pool(name="rawp", bufs=6))
+        grp = ctx.enter_context(tc.tile_pool(name="grp", bufs=6))
+        wqp = ctx.enter_context(tc.tile_pool(name="wqp", bufs=2))
+        outp = ctx.enter_context(tc.tile_pool(name="outp", bufs=12))
+        tmpp = ctx.enter_context(tc.tile_pool(name="tmpp", bufs=4))
+        tps = ctx.enter_context(tc.psum_pool(name="tps", bufs=4))
+        accp = ctx.enter_context(tc.psum_pool(name="accp", bufs=4))
+        ctx.enter_context(tc.manual_schedule())
+
+        raws = {}
+
+        def load_x():
+            raw = rawp.tile([P, 4 * DIM], BF16, name="raw", tag="raw")
+            for b in range(B):
+                nc.sync.dma_start(out=raw[:, b * DIM:(b + 1) * DIM], in_=key_value[b])
+            raws["x"] = raw[:].bitcast(F32)
+
+        def load_w(c, pieces):
+            is_key, idx = CHUNKS[c]
+            w = wk if is_key else wv
+            raw = rawp.tile([P, 4 * DIM], BF16, name="raw", tag="raw")
+            per = 4 // pieces
+            for i in range(pieces):
+                rows = w[idx * 512 + i * per * P: idx * 512 + (i + 1) * per * P, :]
+                nc.sync.dma_start(
+                    out=raw[:, i * per * DIM:(i + 1) * per * DIM].rearrange("p (t k) -> p t k", t=per),
+                    in_=rows.rearrange("(t p) k -> p t k", p=P),
+                )
+            raws[c] = raw[:].bitcast(F32)
+
+        ident = const.tile([P, P], F32, name="ident")
+        make_identity(nc, ident[:])
+        identb = const.tile([P, P], BF16, name="identb")
+        brows = const.tile([P, 512], BF16, name="brows")
+        cos_in = const.tile([P, HD], BF16, name="cos_in")
+        sin_in = const.tile([P, HD], BF16, name="sin_in")
+        cosf = const.tile([P, HD], F32, name="cosf")
+        sinf = const.tile([P, HD], F32, name="sinf")
+        bias_k = const.tile([P, H * HD], F32, name="bias_k")
+        bias_v = const.tile([P, H * HD], F32, name="bias_v")
+        xc = const.tile([P, 4 * 512], U32, name="xc", align_bytes=64)
+        xs = const.tile([P, 4 * 512], U8, name="xs", align_bytes=64)
+
+        nc.vector.memset(brows[:].bitcast(I32), 0)
+        nc.scalar.dma_start(out=brows[0:4, :], in_=bk.rearrange("(r c) -> r c", c=512))
+        nc.scalar.dma_start(out=brows[4:8, :], in_=bv.rearrange("(r c) -> r c", c=512))
+        nc.scalar.dma_start(out=cos_in[:], in_=cos.rearrange("a b s d -> (a b s) d"))
+        nc.scalar.dma_start(out=sin_in[:], in_=sin.rearrange("a b s d -> (a b s) d"))
+        load_x()
+        load_w(0, 4)
+        load_w(1, 2)
+        load_w(2, 2)
+        load_w(3, 2)
+        nc.vector.tensor_copy(out=identb[:], in_=ident[:])
+        nc.vector.tensor_copy(out=cosf[:], in_=cos_in[:])
+        nc.vector.tensor_scalar_mul(out=sinf[:, 0:64], in0=sin_in[:, 0:64], scalar1=-1.0)
+        nc.vector.tensor_copy(out=sinf[:, 64:128], in_=sin_in[:, 64:128])
+        cos_b = cosf[:].unsqueeze(1).to_broadcast([P, 4, HD])
+        sin_lo = sinf[:, 0:64].unsqueeze(1).to_broadcast([P, 4, 64])
+        sin_hi = sinf[:, 64:128].unsqueeze(1).to_broadcast([P, 4, 64])
+
+        def broadcast_bias(row, dst, on_scalar):
+            bank = accp.tile([P, 512], F32, name="acc", tag="acc")
+            nc.tensor.matmul(
+                out=bank[:], lhsT=identb[:, row:row + 1].to_broadcast([P, P]), rhs=brows[:],
+                start=True, stop=True,
+            )
+            if on_scalar:
+                nc.scalar.copy(out=dst, in_=bank[:])
+            else:
+                nc.vector.tensor_copy(out=dst, in_=bank[:])
+
+        def transpose_bank(words, cols):
+            bank = tps.tile([P, 512], F32, name="tbank", tag="tbank")
+            for j in range(4):
+                nc.tensor.transpose(
+                    out=bank[:, j * P:(j + 1) * P], in_=words[:, cols[j]:cols[j] + P], identity=ident[:]
+                )
+            return bank
+
+        def rows_to_grouped(words, t):
+            banks = [transpose_bank(words, [t * 1024 + gp * 512 + j * P for j in range(4)]) for gp in range(2)]
+            grouped = grp.tile([P, 2048], BF16, name="grouped", tag="grouped", align_bytes=64)
+            gw = grouped[:].bitcast(F32)
+            for gp in range(2):
+                nc.scalar.copy(
+                    out=gw[:, gp * 512:(gp + 1) * 512].rearrange("p (g r u) -> p g r u", g=2, u=2),
+                    in_=banks[gp][:].rearrange("p (g u r) -> p g r u", g=2, u=2),
+                )
+            return grouped
+
+        def pass_to_grouped(words, g):
+            banks = [
+                transpose_bank(words, [(2 * fp + (j % 2)) * 1024 + 256 * g + P * (j // 2) for j in range(4)])
+                for fp in range(2)
+            ]
+            grouped = grp.tile([P, 2048], BF16, name="grouped", tag="grouped", align_bytes=64)
+            gw = grouped[:].bitcast(F32)
+            for fp in range(2):
+                nc.scalar.copy(
+                    out=gw[:, fp * 512:(fp + 1) * 512].rearrange("p (f u) -> p f u", u=2),
+                    in_=banks[fp][:].rearrange("p (u f) -> p f u", u=2),
+                )
+            return grouped
+
+        def quantise(grouped, codes, scales, part):
+            cols = slice(part * 512, (part + 1) * 512)
+            nc.vector.quantize_mx(out=codes[:, cols].bitcast(FP8X4), scales=scales[:, cols], in_=grouped[:])
+
+        wq = {}
+
+        def new_wq(c):
+            wc = wqp.tile([P, 4 * 512], U32, name="wc", tag="wc", align_bytes=64)
+            ws = wqp.tile([P, 4 * 512], U8, name="ws", tag="ws", align_bytes=64)
+            wq[c] = (wc, ws)
+
+        def mx(acc_cols, c, b, w_of_g, n):
+            wc, ws = wq[c]
+            for g in range(4):
+                xcols = slice(b * 512 + g * P, b * 512 + (g + 1) * P)
+                wcols = slice(w_of_g(g), w_of_g(g) + n)
+                nc.tensor.matmul_mx(
+                    out=acc_cols,
+                    lhsT=xc[:, xcols].bitcast(FP8X4), lhsT_scale=xs[:, xcols],
+                    rhs=wc[:, wcols].bitcast(FP8X4), rhs_scale=ws[:, wcols],
+                    start=(g == 0), stop=(g == 3),
+                )
+
+        def mx_group(c, b):
+            acc = accp.tile([P, 512], F32, name="acc", tag="acc")
+            mx(acc[:], c, b, lambda g: g * 512, 512)
+            return acc
+
+        deferred = []
+        cursor = [0]
+
+        def run_deferred(n):
+            for i in range(n):
+                if cursor[0] < len(deferred):
+                    deferred[cursor[0]]()
+                    cursor[0] = cursor[0] + 1
+
+        def store(dram, b, idx, o):
+            nc.sync.dma_start(
+                out=dram[b, idx * 4:(idx + 1) * 4, :, :].rearrange("h s d -> s h d"),
+                in_=o[:].rearrange("p (h d) -> p h d", h=4),
+            )
+
+        def evacuate(c, b, acc):
+            is_key, idx = CHUNKS[c]
+            cols = slice(idx * 512, (idx + 1) * 512)
+            if not is_key:
+                o = outp.tile([P, 512], F32, name="o", tag="o")
+                nc.vector.tensor_tensor(out=o[:], in0=acc[:], in1=bias_v[:, cols], op=ADD)
+                store(out_1, b, idx, o)
+                return
+            pb = tmpp.tile([P, 512], F32, name="pb", tag="pb")
+            nc.vector.tensor_tensor(out=pb[:], in0=acc[:], in1=bias_k[:, cols], op=ADD)
+            pbv = pb[:].rearrange("p (h d) -> p h d", h=4)
+            held = {}
+
+            def mul_sin():
+                t2 = tmpp.tile([P, 512], F32, name="t2", tag="t2")
+                t2v = t2[:].rearrange("p (h d) -> p h d", h=4)
+                eng = nc.gpsimd if SIN_ON_GPSIMD else nc.vector
+                eng.tensor_tensor(out=t2v[:, :, 0:64], in0=pbv[:, :, 64:128], in1=sin_lo, op=MULT)
+                eng.tensor_tensor(out=t2v[:, :, 64:128], in0=pbv[:, :, 0:64], in1=sin_hi, op=MULT)
+                held["t2"] = t2
+
+            def mul_cos():
+                o = outp.tile([P, 512], F32, name="o", tag="o")
+                nc.vector.tensor_tensor(
+                    out=o[:].rearrange("p (h d) -> p h d", h=4), in0=pbv, in1=cos_b, op=MULT
+                )
+                held["o"] = o
+
+            def combine():
+                o = held["o"]
+                nc.vector.tensor_tensor(out=o[:], in0=o[:], in1=held["t2"][:], op=ADD)
+                store(out_0, b, idx, o)
+
+            if SIN_ON_GPSIMD:
+                mul_sin()
+                deferred.extend([mul_cos, combine])
+            else:
+                deferred.extend([mul_cos, mul_sin, combine])
+
+        gx = {}
+        gx[0] = rows_to_grouped(raws["x"], 0)
+        gx[1] = rows_to_grouped(raws["x"], 1)
+        quantise(gx[0], xc, xs, 0)
+        for r in range(2):
+            broadcast_bias(r, bias_k[:, r * 512:(r + 1) * 512], False)
+        gx[2] = rows_to_grouped(raws["x"], 2)
+        quantise(gx[1], xc, xs, 1)
+        for r in range(2, 4):
+            broadcast_bias(r, bias_k[:, r * 512:(r + 1) * 512], False)
+        gx[3] = rows_to_grouped(raws["x"], 3)
+        quantise(gx[2], xc, xs, 2)
+        for r in range(2):
+            broadcast_bias(4 + r, bias_v[:, r * 512:(r + 1) * 512], False)
+
+        new_wq(0)
+        wc0, ws0 = wq[0]
+        gw0 = {}
+        acc0 = {}
+
+        def mx_first(f):
+            for b in range(B):
+                if f == 0:
+                    acc0[b] = accp.tile([P, 512], F32, name="acc", tag="acc")
+                mx(acc0[b][:, f * P:(f + 1) * P], 0, b, lambda g: f * 512 + g * P, P)
+
+        gw0[0] = rows_to_grouped(raws[0], 0)
+        quantise(gx[3], xc, xs, 3)
+        for r in range(2, 4):
+            broadcast_bias(4 + r, bias_v[:, r * 512:(r + 1) * 512], False)
+        gw0[1] = rows_to_grouped(raws[0], 1)
+        quantise(gw0[0], wc0, ws0, 0)
+        gw0[2] = rows_to_grouped(raws[0], 2)
+        quantise(gw0[1], wc0, ws0, 1)
+        mx_first(0)
+        gw0[3] = rows_to_grouped(raws[0], 3)
+        quantise(gw0[2], wc0, ws0, 2)
+        mx_first(1)
+        mx_first(2)
+        new_wq(1)
+        wc1, ws1 = wq[1]
+        g10 = pass_to_grouped(raws[1], 0)
+        g11 = pass_to_grouped(raws[1], 1)
+        quantise(gw0[3], wc0, ws0, 3)
+        mx_first(3)
+        quantise(g10, wc1, ws1, 0)
+        evacuate(0, 0, acc0[0])
+        quantise(g11, wc1, ws1, 1)
+        evacuate(0, 1, acc0[1])
+        g12 = pass_to_grouped(raws[1], 2)
+        g13 = pass_to_grouped(raws[1], 3)
+        evacuate(0, 2, acc0[2])
+        evacuate(0, 3, acc0[3])
+        load_w(4, 2)
+        run_deferred(1)
+        quantise(g12, wc1, ws1, 2)
+        run_deferred(1)
+        quantise(g13, wc1, ws1, 3)
+
+        for c in range(1, LAST + 1):
+            more = c < LAST
+            for half in range(2):
+                if more:
+                    if half == 0:
+                        new_wq(c + 1)
+                    wcn, wsn = wq[c + 1]
+                    ga = pass_to_grouped(raws[c + 1], 2 * half)
+                    gb = pass_to_grouped(raws[c + 1], 2 * half + 1)
+                run_deferred(DEFER_A)
+                if more:
+                    quantise(ga, wcn, wsn, 2 * half)
+                acc_a = mx_group(c, 2 * half)
+                acc_b = mx_group(c, 2 * half + 1)
+                run_deferred(DEFER_B)
+                evacuate(c, 2 * half, acc_a)
+                if more:
+                    quantise(gb, wcn, wsn, 2 * half + 1)
+                evacuate(c, 2 * half + 1, acc_b)
+            if c + 4 <= LAST:
+                load_w(c + 4, 2)
+        run_deferred(len(deferred))

@@ -16,9 +16,6 @@ P = 128
 B, S, DIM, H, HD = 4, 128, 2048, 16, 128
 FLOPS = 2 * B * S * DIM * 2 * H * HD
 
-SIN_ON_GPSIMD = False
-DEFER_A = 2
-DEFER_B = 1
 CHUNKS = [(True, 0), (False, 0), (True, 1), (False, 1), (True, 2), (False, 2), (True, 3), (False, 3)]
 LAST = len(CHUNKS) - 1
 
@@ -30,8 +27,8 @@ def tile_attention_pb_kernel(tc, key_value, wk, bk, wv, bv, cos, sin, out_0, out
         rawp = ctx.enter_context(tc.tile_pool(name="rawp", bufs=6))
         grp = ctx.enter_context(tc.tile_pool(name="grp", bufs=6))
         wqp = ctx.enter_context(tc.tile_pool(name="wqp", bufs=2))
-        outp = ctx.enter_context(tc.tile_pool(name="outp", bufs=12))
-        tmpp = ctx.enter_context(tc.tile_pool(name="tmpp", bufs=4))
+        outp = ctx.enter_context(tc.tile_pool(name="outp", bufs=8))
+        keyp = ctx.enter_context(tc.tile_pool(name="keyp", bufs=1))
         tps = ctx.enter_context(tc.psum_pool(name="tps", bufs=4))
         accp = ctx.enter_context(tc.psum_pool(name="accp", bufs=4))
         ctx.enter_context(tc.manual_schedule())
@@ -65,7 +62,7 @@ def tile_attention_pb_kernel(tc, key_value, wk, bk, wv, bv, cos, sin, out_0, out
         sin_in = const.tile([P, HD], BF16, name="sin_in")
         cosf = const.tile([P, HD], F32, name="cosf")
         sinf = const.tile([P, HD], F32, name="sinf")
-        bias_k = const.tile([P, H * HD], F32, name="bias_k")
+        rot_bias = const.tile([P, H * HD], F32, name="rot_bias")
         bias_v = const.tile([P, H * HD], F32, name="bias_v")
         xc = const.tile([P, 4 * 512], U32, name="xc", align_bytes=64)
         xs = const.tile([P, 4 * 512], U8, name="xs", align_bytes=64)
@@ -88,16 +85,30 @@ def tile_attention_pb_kernel(tc, key_value, wk, bk, wv, bv, cos, sin, out_0, out
         sin_lo = sinf[:, 0:64].unsqueeze(1).to_broadcast([P, 4, 64])
         sin_hi = sinf[:, 64:128].unsqueeze(1).to_broadcast([P, 4, 64])
 
-        def broadcast_bias(row, dst, on_scalar):
+        def bias_bank(row):
             bank = accp.tile([P, 512], F32, name="acc", tag="acc")
             nc.tensor.matmul(
                 out=bank[:], lhsT=identb[:, row:row + 1].to_broadcast([P, P]), rhs=brows[:],
                 start=True, stop=True,
             )
-            if on_scalar:
-                nc.scalar.copy(out=dst, in_=bank[:])
-            else:
-                nc.vector.tensor_copy(out=dst, in_=bank[:])
+            return bank
+
+        def rotate_products(bank, straight, crossed):
+            bv4 = bank[:].rearrange("p (h d) -> p h d", h=4)
+            sv4 = straight.rearrange("p (h d) -> p h d", h=4)
+            cv4 = crossed.rearrange("p (h d) -> p h d", h=4)
+            nc.vector.tensor_tensor(out=sv4, in0=bv4, in1=cos_b, op=MULT)
+            nc.vector.tensor_tensor(out=cv4[:, :, 0:64], in0=bv4[:, :, 64:128], in1=sin_lo, op=MULT)
+            nc.vector.tensor_tensor(out=cv4[:, :, 64:128], in0=bv4[:, :, 0:64], in1=sin_hi, op=MULT)
+
+        def key_bias(r):
+            cols = slice(r * 512, (r + 1) * 512)
+            crossed = keyp.tile([P, 1024], F32, name="crossed", tag="crossed", bufs=3)
+            rotate_products(bias_bank(r), rot_bias[:, cols], crossed[:, 0:512])
+            nc.gpsimd.tensor_tensor(out=rot_bias[:, cols], in0=rot_bias[:, cols], in1=crossed[:, 0:512], op=ADD)
+
+        def value_bias(r):
+            nc.vector.tensor_copy(out=bias_v[:, r * 512:(r + 1) * 512], in_=bias_bank(4 + r)[:])
 
         def transpose_bank(words, cols):
             bank = tps.tile([P, 512], F32, name="tbank", tag="tbank")
@@ -160,20 +171,21 @@ def tile_attention_pb_kernel(tc, key_value, wk, bk, wv, bv, cos, sin, out_0, out
             mx(acc[:], c, b, lambda g: g * 512, 512)
             return acc
 
-        deferred = []
-        cursor = [0]
-
-        def run_deferred(n):
-            for i in range(n):
-                if cursor[0] < len(deferred):
-                    deferred[cursor[0]]()
-                    cursor[0] = cursor[0] + 1
-
         def store(dram, b, idx, o):
             nc.sync.dma_start(
                 out=dram[b, idx * 4:(idx + 1) * 4, :, :].rearrange("h s d -> s h d"),
-                in_=o[:].rearrange("p (h d) -> p h d", h=4),
+                in_=o.rearrange("p (h d) -> p h d", h=4),
             )
+
+        late_stores = []
+        sent = [0]
+        clock = [-1]
+        held = {}
+
+        def flush_stores():
+            while sent[0] < len(late_stores) and late_stores[sent[0]][0] <= clock[0]:
+                late_stores[sent[0]][1]()
+                sent[0] = sent[0] + 1
 
         def evacuate(c, b, acc):
             is_key, idx = CHUNKS[c]
@@ -181,53 +193,42 @@ def tile_attention_pb_kernel(tc, key_value, wk, bk, wv, bv, cos, sin, out_0, out
             if not is_key:
                 o = outp.tile([P, 512], F32, name="o", tag="o")
                 nc.vector.tensor_tensor(out=o[:], in0=acc[:], in1=bias_v[:, cols], op=ADD)
-                store(out_1, b, idx, o)
+                store(out_1, b, idx, o[:])
                 return
-            pb = tmpp.tile([P, 512], F32, name="pb", tag="pb")
-            nc.vector.tensor_tensor(out=pb[:], in0=acc[:], in1=bias_k[:, cols], op=ADD)
-            pbv = pb[:].rearrange("p (h d) -> p h d", h=4)
-            held = {}
-
-            def mul_sin():
-                t2 = tmpp.tile([P, 512], F32, name="t2", tag="t2")
-                t2v = t2[:].rearrange("p (h d) -> p h d", h=4)
-                eng = nc.gpsimd if SIN_ON_GPSIMD else nc.vector
-                eng.tensor_tensor(out=t2v[:, :, 0:64], in0=pbv[:, :, 64:128], in1=sin_lo, op=MULT)
-                eng.tensor_tensor(out=t2v[:, :, 64:128], in0=pbv[:, :, 0:64], in1=sin_hi, op=MULT)
-                held["t2"] = t2
-
-            def mul_cos():
-                o = outp.tile([P, 512], F32, name="o", tag="o")
-                nc.vector.tensor_tensor(
-                    out=o[:].rearrange("p (h d) -> p h d", h=4), in0=pbv, in1=cos_b, op=MULT
+            i = b % 2
+            if i == 0:
+                held["s"] = keyp.tile([P, 1024], F32, name="straight", tag="straight", bufs=6)
+                held["c"] = keyp.tile([P, 1024], F32, name="crossed", tag="crossed", bufs=3)
+            straight = held["s"]
+            crossed = held["c"]
+            rotate_products(acc, straight[:, i * 512:(i + 1) * 512], crossed[:, i * 512:(i + 1) * 512])
+            if i == 1:
+                nc.gpsimd.tensor_tensor(out=straight[:], in0=straight[:], in1=crossed[:], op=ADD)
+                pair = straight[:].rearrange("p (b f) -> p b f", b=2)
+                nc.gpsimd.tensor_tensor(
+                    out=pair, in0=pair, in1=rot_bias[:, cols].unsqueeze(1).to_broadcast([P, 2, 512]), op=ADD
                 )
-                held["o"] = o
 
-            def combine():
-                o = held["o"]
-                nc.vector.tensor_tensor(out=o[:], in0=o[:], in1=held["t2"][:], op=ADD)
-                store(out_0, b, idx, o)
+                def both():
+                    store(out_0, b - 1, idx, straight[:, 0:512])
+                    store(out_0, b, idx, straight[:, 512:1024])
 
-            if SIN_ON_GPSIMD:
-                mul_sin()
-                deferred.extend([mul_cos, combine])
-            else:
-                deferred.extend([mul_cos, mul_sin, combine])
+                late_stores.append((clock[0] + 2, both))
 
         gx = {}
         gx[0] = rows_to_grouped(raws["x"], 0)
         gx[1] = rows_to_grouped(raws["x"], 1)
         quantise(gx[0], xc, xs, 0)
-        for r in range(2):
-            broadcast_bias(r, bias_k[:, r * 512:(r + 1) * 512], False)
+        key_bias(0)
+        key_bias(1)
         gx[2] = rows_to_grouped(raws["x"], 2)
         quantise(gx[1], xc, xs, 1)
-        for r in range(2, 4):
-            broadcast_bias(r, bias_k[:, r * 512:(r + 1) * 512], False)
+        key_bias(2)
+        key_bias(3)
         gx[3] = rows_to_grouped(raws["x"], 3)
         quantise(gx[2], xc, xs, 2)
-        for r in range(2):
-            broadcast_bias(4 + r, bias_v[:, r * 512:(r + 1) * 512], False)
+        value_bias(0)
+        value_bias(1)
 
         new_wq(0)
         wc0, ws0 = wq[0]
@@ -242,8 +243,8 @@ def tile_attention_pb_kernel(tc, key_value, wk, bk, wv, bv, cos, sin, out_0, out
 
         gw0[0] = rows_to_grouped(raws[0], 0)
         quantise(gx[3], xc, xs, 3)
-        for r in range(2, 4):
-            broadcast_bias(4 + r, bias_v[:, r * 512:(r + 1) * 512], False)
+        value_bias(2)
+        value_bias(3)
         gw0[1] = rows_to_grouped(raws[0], 1)
         quantise(gw0[0], wc0, ws0, 0)
         gw0[2] = rows_to_grouped(raws[0], 2)
@@ -265,12 +266,11 @@ def tile_attention_pb_kernel(tc, key_value, wk, bk, wv, bv, cos, sin, out_0, out
         evacuate(0, 1, acc0[1])
         g12 = pass_to_grouped(raws[1], 2)
         g13 = pass_to_grouped(raws[1], 3)
+        clock[0] = 0
         evacuate(0, 2, acc0[2])
         evacuate(0, 3, acc0[3])
         load_w(4, 2)
-        run_deferred(1)
         quantise(g12, wc1, ws1, 2)
-        run_deferred(1)
         quantise(g13, wc1, ws1, 3)
 
         for c in range(1, LAST + 1):
@@ -282,16 +282,17 @@ def tile_attention_pb_kernel(tc, key_value, wk, bk, wv, bv, cos, sin, out_0, out
                     wcn, wsn = wq[c + 1]
                     ga = pass_to_grouped(raws[c + 1], 2 * half)
                     gb = pass_to_grouped(raws[c + 1], 2 * half + 1)
-                run_deferred(DEFER_A)
                 if more:
                     quantise(ga, wcn, wsn, 2 * half)
                 acc_a = mx_group(c, 2 * half)
                 acc_b = mx_group(c, 2 * half + 1)
-                run_deferred(DEFER_B)
+                clock[0] = clock[0] + 1
+                flush_stores()
                 evacuate(c, 2 * half, acc_a)
                 if more:
                     quantise(gb, wcn, wsn, 2 * half + 1)
                 evacuate(c, 2 * half + 1, acc_b)
             if c + 4 <= LAST:
                 load_w(c + 4, 2)
-        run_deferred(len(deferred))
+        clock[0] = clock[0] + 2
+        flush_stores()

@@ -62,7 +62,7 @@ def tile_attention_pb_kernel(tc, key_value, wk, bk, wv, bv, cos, sin, out_0, out
         sin_in = const.tile([P, HD], BF16, name="sin_in")
         cosf = const.tile([P, HD], F32, name="cosf")
         sinf = const.tile([P, HD], F32, name="sinf")
-        rot_bias = const.tile([P, H * HD], F32, name="rot_bias")
+        bias_k = const.tile([P, H * HD], F32, name="bias_k")
         bias_v = const.tile([P, H * HD], F32, name="bias_v")
         xc = const.tile([P, 4 * 512], U32, name="xc", align_bytes=64)
         xs = const.tile([P, 4 * 512], U8, name="xs", align_bytes=64)
@@ -81,34 +81,20 @@ def tile_attention_pb_kernel(tc, key_value, wk, bk, wv, bv, cos, sin, out_0, out
         nc.vector.tensor_copy(out=cosf[:], in_=cos_in[:])
         nc.vector.tensor_scalar_mul(out=sinf[:, 0:64], in0=sin_in[:, 0:64], scalar1=-1.0)
         nc.vector.tensor_copy(out=sinf[:, 64:128], in_=sin_in[:, 64:128])
-        cos_b = cosf[:].unsqueeze(1).to_broadcast([P, 4, HD])
-        sin_lo = sinf[:, 0:64].unsqueeze(1).to_broadcast([P, 4, 64])
-        sin_hi = sinf[:, 64:128].unsqueeze(1).to_broadcast([P, 4, 64])
+        cos_b = cosf[:].unsqueeze(1).to_broadcast([P, 8, HD])
+        sin_lo = sinf[:, 0:64].unsqueeze(1).to_broadcast([P, 8, 64])
+        sin_hi = sinf[:, 64:128].unsqueeze(1).to_broadcast([P, 8, 64])
 
-        def bias_bank(row):
+        def broadcast_bias(row, dst, on_scalar):
             bank = accp.tile([P, 512], F32, name="acc", tag="acc")
             nc.tensor.matmul(
                 out=bank[:], lhsT=identb[:, row:row + 1].to_broadcast([P, P]), rhs=brows[:],
                 start=True, stop=True,
             )
-            return bank
-
-        def rotate_products(bank, straight, crossed):
-            bv4 = bank[:].rearrange("p (h d) -> p h d", h=4)
-            sv4 = straight.rearrange("p (h d) -> p h d", h=4)
-            cv4 = crossed.rearrange("p (h d) -> p h d", h=4)
-            nc.vector.tensor_tensor(out=sv4, in0=bv4, in1=cos_b, op=MULT)
-            nc.vector.tensor_tensor(out=cv4[:, :, 0:64], in0=bv4[:, :, 64:128], in1=sin_lo, op=MULT)
-            nc.vector.tensor_tensor(out=cv4[:, :, 64:128], in0=bv4[:, :, 0:64], in1=sin_hi, op=MULT)
-
-        def key_bias(r):
-            cols = slice(r * 512, (r + 1) * 512)
-            crossed = keyp.tile([P, 1024], F32, name="crossed", tag="crossed", bufs=3)
-            rotate_products(bias_bank(r), rot_bias[:, cols], crossed[:, 0:512])
-            nc.gpsimd.tensor_tensor(out=rot_bias[:, cols], in0=rot_bias[:, cols], in1=crossed[:, 0:512], op=ADD)
-
-        def value_bias(r):
-            nc.vector.tensor_copy(out=bias_v[:, r * 512:(r + 1) * 512], in_=bias_bank(4 + r)[:])
+            if on_scalar:
+                nc.scalar.copy(out=dst, in_=bank[:])
+            else:
+                nc.vector.tensor_copy(out=dst, in_=bank[:])
 
         def transpose_bank(words, cols):
             bank = tps.tile([P, 512], F32, name="tbank", tag="tbank")
@@ -171,64 +157,101 @@ def tile_attention_pb_kernel(tc, key_value, wk, bk, wv, bv, cos, sin, out_0, out
             mx(acc[:], c, b, lambda g: g * 512, 512)
             return acc
 
-        def store(dram, b, idx, o):
+        deferred = []
+        cursor = [0]
+
+        def run_deferred(n):
+            for i in range(n):
+                if cursor[0] < len(deferred):
+                    deferred[cursor[0]]()
+                    cursor[0] = cursor[0] + 1
+
+        def store_heads(dram, b, idx, o):
             nc.sync.dma_start(
                 out=dram[b, idx * 4:(idx + 1) * 4, :, :].rearrange("h s d -> s h d"),
                 in_=o.rearrange("p (h d) -> p h d", h=4),
             )
 
-        late_stores = []
-        sent = [0]
-        clock = [-1]
+        def store_batches(dram, h, o):
+            nc.sync.dma_start(
+                out=dram[:, h, :, :].rearrange("b s d -> s b d"),
+                in_=o.rearrange("p (b d) -> p b d", b=4),
+            )
+
         held = {}
 
-        def flush_stores():
-            while sent[0] < len(late_stores) and late_stores[sent[0]][0] <= clock[0]:
-                late_stores[sent[0]][1]()
-                sent[0] = sent[0] + 1
+        def evacuate_key(i, acc, bias, store_it):
+            if i == 0:
+                held["pb"] = keyp.tile([P, 1024], F32, name="pb", tag="pb", bufs=4)
+                held["stores"] = []
+            pb = held["pb"]
+            stores = held["stores"]
+            stores.append(store_it)
+            nc.vector.tensor_tensor(
+                out=pb[:, i * 512:(i + 1) * 512].rearrange("p (a d) -> p a d", a=4),
+                in0=acc[:].rearrange("p (a d) -> p a d", a=4), in1=bias, op=ADD,
+            )
+            if i == 0:
+                return
+            pbv = pb[:].rearrange("p (a d) -> p a d", a=8)
+            mine = {}
+
+            def mul_cos():
+                mine["o"] = keyp.tile([P, 1024], F32, name="ko", tag="ko", bufs=4)
+                nc.vector.tensor_tensor(
+                    out=mine["o"][:].rearrange("p (a d) -> p a d", a=8), in0=pbv, in1=cos_b, op=MULT
+                )
+
+            def mul_sin_lo():
+                mine["x"] = keyp.tile([P, 1024], F32, name="kx", tag="kx", bufs=2)
+                xv = mine["x"][:].rearrange("p (a d) -> p a d", a=8)
+                nc.vector.tensor_tensor(out=xv[:, :, 0:64], in0=pbv[:, :, 64:128], in1=sin_lo, op=MULT)
+
+            def mul_sin_hi():
+                xv = mine["x"][:].rearrange("p (a d) -> p a d", a=8)
+                nc.vector.tensor_tensor(out=xv[:, :, 64:128], in0=pbv[:, :, 0:64], in1=sin_hi, op=MULT)
+
+            def combine():
+                o = mine["o"]
+                nc.vector.tensor_tensor(out=o[:], in0=o[:], in1=mine["x"][:], op=ADD)
+                stores[0](o[:, 0:512])
+                stores[1](o[:, 512:1024])
+
+            deferred.extend([mul_cos, mul_sin_lo, mul_sin_hi, combine])
 
         def evacuate(c, b, acc):
             is_key, idx = CHUNKS[c]
             cols = slice(idx * 512, (idx + 1) * 512)
-            if not is_key:
+            if is_key:
+                evacuate_key(
+                    b % 2, acc, bias_k[:, cols].rearrange("p (a d) -> p a d", a=4),
+                    lambda o: store_heads(out_0, b, idx, o),
+                )
+            else:
                 o = outp.tile([P, 512], F32, name="o", tag="o")
                 nc.vector.tensor_tensor(out=o[:], in0=acc[:], in1=bias_v[:, cols], op=ADD)
-                store(out_1, b, idx, o[:])
-                return
-            i = b % 2
-            if i == 0:
-                held["s"] = keyp.tile([P, 1024], F32, name="straight", tag="straight", bufs=6)
-                held["c"] = keyp.tile([P, 1024], F32, name="crossed", tag="crossed", bufs=3)
-            straight = held["s"]
-            crossed = held["c"]
-            rotate_products(acc, straight[:, i * 512:(i + 1) * 512], crossed[:, i * 512:(i + 1) * 512])
-            if i == 1:
-                nc.gpsimd.tensor_tensor(out=straight[:], in0=straight[:], in1=crossed[:], op=ADD)
-                pair = straight[:].rearrange("p (b f) -> p b f", b=2)
-                nc.gpsimd.tensor_tensor(
-                    out=pair, in0=pair, in1=rot_bias[:, cols].unsqueeze(1).to_broadcast([P, 2, 512]), op=ADD
-                )
+                store_heads(out_1, b, idx, o[:])
 
-                def both():
-                    store(out_0, b - 1, idx, straight[:, 0:512])
-                    store(out_0, b, idx, straight[:, 512:1024])
-
-                late_stores.append((clock[0] + 2, both))
+        def evacuate_first(f, acc):
+            evacuate_key(
+                f % 2, acc, bias_k[:, f * HD:(f + 1) * HD].unsqueeze(1).to_broadcast([P, 4, HD]),
+                lambda o: store_batches(out_0, f, o),
+            )
 
         gx = {}
         gx[0] = rows_to_grouped(raws["x"], 0)
         gx[1] = rows_to_grouped(raws["x"], 1)
         quantise(gx[0], xc, xs, 0)
-        key_bias(0)
-        key_bias(1)
+        for r in range(2):
+            broadcast_bias(r, bias_k[:, r * 512:(r + 1) * 512], False)
         gx[2] = rows_to_grouped(raws["x"], 2)
         quantise(gx[1], xc, xs, 1)
-        key_bias(2)
-        key_bias(3)
+        for r in range(2, 4):
+            broadcast_bias(r, bias_k[:, r * 512:(r + 1) * 512], False)
         gx[3] = rows_to_grouped(raws["x"], 3)
         quantise(gx[2], xc, xs, 2)
-        value_bias(0)
-        value_bias(1)
+        for r in range(2):
+            broadcast_bias(4 + r, bias_v[:, r * 512:(r + 1) * 512], False)
 
         new_wq(0)
         wc0, ws0 = wq[0]
@@ -236,15 +259,14 @@ def tile_attention_pb_kernel(tc, key_value, wk, bk, wv, bv, cos, sin, out_0, out
         acc0 = {}
 
         def mx_first(f):
+            acc0[f] = accp.tile([P, 512], F32, name="acc", tag="acc")
             for b in range(B):
-                if f == 0:
-                    acc0[b] = accp.tile([P, 512], F32, name="acc", tag="acc")
-                mx(acc0[b][:, f * P:(f + 1) * P], 0, b, lambda g: f * 512 + g * P, P)
+                mx(acc0[f][:, b * P:(b + 1) * P], 0, b, lambda g: f * 512 + g * P, P)
 
         gw0[0] = rows_to_grouped(raws[0], 0)
         quantise(gx[3], xc, xs, 3)
-        value_bias(2)
-        value_bias(3)
+        for r in range(2, 4):
+            broadcast_bias(4 + r, bias_v[:, r * 512:(r + 1) * 512], False)
         gw0[1] = rows_to_grouped(raws[0], 1)
         quantise(gw0[0], wc0, ws0, 0)
         gw0[2] = rows_to_grouped(raws[0], 2)
@@ -252,26 +274,29 @@ def tile_attention_pb_kernel(tc, key_value, wk, bk, wv, bv, cos, sin, out_0, out
         mx_first(0)
         gw0[3] = rows_to_grouped(raws[0], 3)
         quantise(gw0[2], wc0, ws0, 2)
+        evacuate_first(0, acc0[0])
         mx_first(1)
+        evacuate_first(1, acc0[1])
         mx_first(2)
         new_wq(1)
         wc1, ws1 = wq[1]
         g10 = pass_to_grouped(raws[1], 0)
         g11 = pass_to_grouped(raws[1], 1)
         quantise(gw0[3], wc0, ws0, 3)
+        run_deferred(1)
+        evacuate_first(2, acc0[2])
         mx_first(3)
         quantise(g10, wc1, ws1, 0)
-        evacuate(0, 0, acc0[0])
+        run_deferred(1)
+        evacuate_first(3, acc0[3])
         quantise(g11, wc1, ws1, 1)
-        evacuate(0, 1, acc0[1])
         g12 = pass_to_grouped(raws[1], 2)
         g13 = pass_to_grouped(raws[1], 3)
-        clock[0] = 0
-        evacuate(0, 2, acc0[2])
-        evacuate(0, 3, acc0[3])
-        load_w(4, 2)
+        run_deferred(1)
         quantise(g12, wc1, ws1, 2)
+        run_deferred(1)
         quantise(g13, wc1, ws1, 3)
+        load_w(4, 2)
 
         for c in range(1, LAST + 1):
             more = c < LAST
@@ -282,17 +307,16 @@ def tile_attention_pb_kernel(tc, key_value, wk, bk, wv, bv, cos, sin, out_0, out
                     wcn, wsn = wq[c + 1]
                     ga = pass_to_grouped(raws[c + 1], 2 * half)
                     gb = pass_to_grouped(raws[c + 1], 2 * half + 1)
+                run_deferred(1 if more else 2)
                 if more:
                     quantise(ga, wcn, wsn, 2 * half)
                 acc_a = mx_group(c, 2 * half)
                 acc_b = mx_group(c, 2 * half + 1)
-                clock[0] = clock[0] + 1
-                flush_stores()
                 evacuate(c, 2 * half, acc_a)
+                run_deferred(1 if more else 2)
                 if more:
                     quantise(gb, wcn, wsn, 2 * half + 1)
                 evacuate(c, 2 * half + 1, acc_b)
             if c + 4 <= LAST:
                 load_w(c + 4, 2)
-        clock[0] = clock[0] + 2
-        flush_stores()
+        run_deferred(len(deferred))

@@ -31,7 +31,6 @@ def tile_attention_pb_kernel(tc, key_value, wk, bk, wv, bv, cos, sin, out_0, out
         keyp = ctx.enter_context(tc.tile_pool(name="keyp", bufs=1))
         tps = ctx.enter_context(tc.psum_pool(name="tps", bufs=4))
         accp = ctx.enter_context(tc.psum_pool(name="accp", bufs=4))
-        ctx.enter_context(tc.manual_schedule())
 
         raws = {}
 

@@ -14,308 +14,298 @@ MULT = mybir.AluOpType.mult
 
 P = 128
 B, S, DIM, H, HD = 4, 128, 2048, 16, 128
+HALF = HD // 2
+PASSES = DIM // (4 * P)
+WORDS = DIM // 2
+PASS_WORDS = WORDS // PASSES
+BANK = 512
+BLOCK = BANK
+TILES = BLOCK // P
+HEADS = BLOCK // HD
+BIAS_ROWS = H * HD // BLOCK
+RUN = 4
+QWORDS = DIM // 4
 FLOPS = 2 * B * S * DIM * 2 * H * HD
 
-CHUNKS = [(True, 0), (False, 0), (True, 1), (False, 1), (True, 2), (False, 2), (True, 3), (False, 3)]
-LAST = len(CHUNKS) - 1
+BLOCKS = [(True, 0), (False, 0), (True, 1), (False, 1), (True, 2), (False, 2), (True, 3), (False, 3)]
+LAST = len(BLOCKS) - 1
+LOADS_AHEAD = 4
+DEFERRED_BEFORE_QUANTISE = 2
+DEFERRED_AFTER_MATMULS = 1
 
 
 def tile_attention_pb_kernel(tc, key_value, wk, bk, wv, bv, cos, sin, out_0, out_1):
     nc = tc.nc
     with ExitStack() as ctx:
         const = ctx.enter_context(tc.tile_pool(name="const", bufs=1))
-        rawp = ctx.enter_context(tc.tile_pool(name="rawp", bufs=6))
+        rawp = ctx.enter_context(tc.tile_pool(name="rawp", bufs=LOADS_AHEAD + 2))
         grp = ctx.enter_context(tc.tile_pool(name="grp", bufs=6))
         wqp = ctx.enter_context(tc.tile_pool(name="wqp", bufs=2))
-        outp = ctx.enter_context(tc.tile_pool(name="outp", bufs=8))
-        keyp = ctx.enter_context(tc.tile_pool(name="keyp", bufs=1))
+        outp = ctx.enter_context(tc.tile_pool(name="outp", bufs=4))
+        tmpp = ctx.enter_context(tc.tile_pool(name="tmpp", bufs=4))
         tps = ctx.enter_context(tc.psum_pool(name="tps", bufs=4))
         accp = ctx.enter_context(tc.psum_pool(name="accp", bufs=4))
+        ctx.enter_context(tc.manual_schedule())
 
-        raws = {}
+        raw_words = {}
 
-        def load_x():
-            raw = rawp.tile([P, 4 * DIM], BF16, name="raw", tag="raw")
+        def load_activations():
+            raw = rawp.tile([P, B * DIM], BF16, name="raw", tag="raw")
             for b in range(B):
-                nc.sync.dma_start(out=raw[:, b * DIM:(b + 1) * DIM], in_=key_value[b])
-            raws["x"] = raw[:].bitcast(F32)
+                nc.sync.dma_start(out=raw[b:P:B, :], in_=key_value[b].rearrange("(j e) k -> j (e k)", e=RUN))
+            raw_words["x"] = raw[:].bitcast(F32)
 
-        def load_w(c, pieces):
-            is_key, idx = CHUNKS[c]
+        def load_weights(c, pieces):
+            is_key, idx = BLOCKS[c]
             w = wk if is_key else wv
-            raw = rawp.tile([P, 4 * DIM], BF16, name="raw", tag="raw")
-            per = 4 // pieces
+            raw = rawp.tile([P, TILES * DIM], BF16, name="raw", tag="raw")
+            per = TILES // pieces
             for i in range(pieces):
-                rows = w[idx * 512 + i * per * P: idx * 512 + (i + 1) * per * P, :]
+                rows = w[idx * BLOCK + i * per * P: idx * BLOCK + (i + 1) * per * P, :]
                 nc.sync.dma_start(
                     out=raw[:, i * per * DIM:(i + 1) * per * DIM].rearrange("p (t k) -> p t k", t=per),
                     in_=rows.rearrange("(t p) k -> p t k", p=P),
                 )
-            raws[c] = raw[:].bitcast(F32)
+            raw_words[c] = raw[:].bitcast(F32)
 
         ident = const.tile([P, P], F32, name="ident")
         make_identity(nc, ident[:])
         identb = const.tile([P, P], BF16, name="identb")
-        brows = const.tile([P, 512], BF16, name="brows")
-        cos_in = const.tile([P, HD], BF16, name="cos_in")
-        sin_in = const.tile([P, HD], BF16, name="sin_in")
-        cosf = const.tile([P, HD], F32, name="cosf")
-        sinf = const.tile([P, HD], F32, name="sinf")
+        brows = const.tile([P, BLOCK], BF16, name="brows")
+        cos_in = const.tile([P, RUN * HD], BF16, name="cos_in")
+        sin_in = const.tile([P, RUN * HD], BF16, name="sin_in")
+        cosf = const.tile([P, RUN * HD], F32, name="cosf")
+        sinf = const.tile([P, RUN * HD], F32, name="sinf")
         bias_k = const.tile([P, H * HD], F32, name="bias_k")
         bias_v = const.tile([P, H * HD], F32, name="bias_v")
-        xc = const.tile([P, 4 * 512], U32, name="xc", align_bytes=64)
-        xs = const.tile([P, 4 * 512], U8, name="xs", align_bytes=64)
+        xc = const.tile([P, B * QWORDS], U32, name="xc", align_bytes=64)
+        xs = const.tile([P, B * QWORDS], U8, name="xs", align_bytes=64)
 
         nc.vector.memset(brows[:].bitcast(I32), 0)
-        nc.scalar.dma_start(out=brows[0:4, :], in_=bk.rearrange("(r c) -> r c", c=512))
-        nc.scalar.dma_start(out=brows[4:8, :], in_=bv.rearrange("(r c) -> r c", c=512))
-        nc.scalar.dma_start(out=cos_in[:], in_=cos.rearrange("a b s d -> (a b s) d"))
-        nc.scalar.dma_start(out=sin_in[:], in_=sin.rearrange("a b s d -> (a b s) d"))
-        load_x()
-        load_w(0, 4)
-        load_w(1, 2)
-        load_w(2, 2)
-        load_w(3, 2)
+        nc.scalar.dma_start(out=brows[0:BIAS_ROWS, :], in_=bk.rearrange("(r c) -> r c", c=BLOCK))
+        nc.scalar.dma_start(out=brows[BIAS_ROWS:2 * BIAS_ROWS, :], in_=bv.rearrange("(r c) -> r c", c=BLOCK))
+        for b in range(B):
+            nc.gpsimd.dma_start(out=cos_in[b:P:B, :], in_=cos.rearrange("a b (j e) d -> (a b j) (e d)", e=RUN))
+            nc.gpsimd.dma_start(out=sin_in[b:P:B, :], in_=sin.rearrange("a b (j e) d -> (a b j) (e d)", e=RUN))
+        load_activations()
+        load_weights(0, TILES)
+        for c in range(1, LOADS_AHEAD):
+            load_weights(c, 2)
         nc.vector.tensor_copy(out=identb[:], in_=ident[:])
-        nc.vector.tensor_copy(out=cosf[:], in_=cos_in[:])
-        nc.vector.tensor_scalar_mul(out=sinf[:, 0:64], in0=sin_in[:, 0:64], scalar1=-1.0)
-        nc.vector.tensor_copy(out=sinf[:, 64:128], in_=sin_in[:, 64:128])
-        cos_b = cosf[:].unsqueeze(1).to_broadcast([P, 8, HD])
-        sin_lo = sinf[:, 0:64].unsqueeze(1).to_broadcast([P, 8, 64])
-        sin_hi = sinf[:, 64:128].unsqueeze(1).to_broadcast([P, 8, 64])
 
-        def broadcast_bias(row, dst, on_scalar):
-            bank = accp.tile([P, 512], F32, name="acc", tag="acc")
+        def make_tables():
+            sin_v = sin_in[:].rearrange("p (e d) -> p e d", e=RUN)
+            sinf_v = sinf[:].rearrange("p (e d) -> p e d", e=RUN)
+            nc.vector.tensor_copy(out=cosf[:], in_=cos_in[:])
+            nc.vector.tensor_scalar_mul(out=sinf_v[:, :, 0:HALF], in0=sin_v[:, :, 0:HALF], scalar1=-1.0)
+            nc.vector.tensor_copy(out=sinf_v[:, :, HALF:HD], in_=sin_v[:, :, HALF:HD])
+
+        def table(t, e, lo, hi):
+            return t[:, e * HD + lo:e * HD + hi].unsqueeze(1).to_broadcast([P, HEADS, hi - lo])
+
+        def broadcast_bias(row, dst):
+            bank = accp.tile([P, BANK], F32, name="acc", tag="acc")
             nc.tensor.matmul(
                 out=bank[:], lhsT=identb[:, row:row + 1].to_broadcast([P, P]), rhs=brows[:],
                 start=True, stop=True,
             )
-            if on_scalar:
-                nc.scalar.copy(out=dst, in_=bank[:])
-            else:
-                nc.vector.tensor_copy(out=dst, in_=bank[:])
+            nc.vector.tensor_copy(out=dst, in_=bank[:])
 
         def transpose_bank(words, cols):
-            bank = tps.tile([P, 512], F32, name="tbank", tag="tbank")
+            bank = tps.tile([P, BANK], F32, name="tbank", tag="tbank")
             for j in range(4):
                 nc.tensor.transpose(
                     out=bank[:, j * P:(j + 1) * P], in_=words[:, cols[j]:cols[j] + P], identity=ident[:]
                 )
             return bank
 
-        def rows_to_grouped(words, t):
-            banks = [transpose_bank(words, [t * 1024 + gp * 512 + j * P for j in range(4)]) for gp in range(2)]
-            grouped = grp.tile([P, 2048], BF16, name="grouped", tag="grouped", align_bytes=64)
+        def rows_to_grouped(words, t, share=False):
+            banks = [transpose_bank(words, [t * WORDS + (4 * gp + j) * P for j in range(4)]) for gp in range(2)]
+            grouped = grp.tile([P, DIM], BF16, name="grouped", tag="grouped", align_bytes=64)
             gw = grouped[:].bitcast(F32)
             for gp in range(2):
-                nc.scalar.copy(
-                    out=gw[:, gp * 512:(gp + 1) * 512].rearrange("p (g r u) -> p g r u", g=2, u=2),
+                copy = nc.vector.tensor_copy if (share and gp == 1) else nc.scalar.copy
+                copy(
+                    out=gw[:, gp * BANK:(gp + 1) * BANK].rearrange("p (g r u) -> p g r u", g=2, u=2),
                     in_=banks[gp][:].rearrange("p (g u r) -> p g r u", g=2, u=2),
                 )
             return grouped
 
         def pass_to_grouped(words, g):
             banks = [
-                transpose_bank(words, [(2 * fp + (j % 2)) * 1024 + 256 * g + P * (j // 2) for j in range(4)])
+                transpose_bank(words, [(2 * fp + (j % 2)) * WORDS + PASS_WORDS * g + P * (j // 2) for j in range(4)])
                 for fp in range(2)
             ]
-            grouped = grp.tile([P, 2048], BF16, name="grouped", tag="grouped", align_bytes=64)
+            grouped = grp.tile([P, DIM], BF16, name="grouped", tag="grouped", align_bytes=64)
             gw = grouped[:].bitcast(F32)
             for fp in range(2):
                 nc.scalar.copy(
-                    out=gw[:, fp * 512:(fp + 1) * 512].rearrange("p (f u) -> p f u", u=2),
+                    out=gw[:, fp * BANK:(fp + 1) * BANK].rearrange("p (f u) -> p f u", u=2),
                     in_=banks[fp][:].rearrange("p (u f) -> p f u", u=2),
                 )
             return grouped
 
         def quantise(grouped, codes, scales, part):
-            cols = slice(part * 512, (part + 1) * 512)
+            cols = slice(part * QWORDS, (part + 1) * QWORDS)
             nc.vector.quantize_mx(out=codes[:, cols].bitcast(FP8X4), scales=scales[:, cols], in_=grouped[:])
 
-        wq = {}
+        quantised = {}
 
-        def new_wq(c):
-            wc = wqp.tile([P, 4 * 512], U32, name="wc", tag="wc", align_bytes=64)
-            ws = wqp.tile([P, 4 * 512], U8, name="ws", tag="ws", align_bytes=64)
-            wq[c] = (wc, ws)
+        def new_quantised(c):
+            wc = wqp.tile([P, PASSES * QWORDS], U32, name="wc", tag="wc", align_bytes=64)
+            ws = wqp.tile([P, PASSES * QWORDS], U8, name="ws", tag="ws", align_bytes=64)
+            quantised[c] = (wc, ws)
 
-        def mx(acc_cols, c, b, w_of_g, n):
-            wc, ws = wq[c]
-            for g in range(4):
-                xcols = slice(b * 512 + g * P, b * 512 + (g + 1) * P)
-                wcols = slice(w_of_g(g), w_of_g(g) + n)
+        def multiply(acc_cols, c, b, first_col, n):
+            wc, ws = quantised[c]
+            for g in range(PASSES):
+                xcols = slice(b * QWORDS + g * P, b * QWORDS + (g + 1) * P)
+                wcols = slice(first_col(g), first_col(g) + n)
                 nc.tensor.matmul_mx(
                     out=acc_cols,
                     lhsT=xc[:, xcols].bitcast(FP8X4), lhsT_scale=xs[:, xcols],
                     rhs=wc[:, wcols].bitcast(FP8X4), rhs_scale=ws[:, wcols],
-                    start=(g == 0), stop=(g == 3),
+                    start=(g == 0), stop=(g == PASSES - 1),
                 )
 
-        def mx_group(c, b):
-            acc = accp.tile([P, 512], F32, name="acc", tag="acc")
-            mx(acc[:], c, b, lambda g: g * 512, 512)
+        def multiply_block(c, b):
+            acc = accp.tile([P, BANK], F32, name="acc", tag="acc")
+            multiply(acc[:], c, b, lambda g: g * QWORDS, BLOCK)
             return acc
 
         deferred = []
-        cursor = [0]
+        done = [0]
 
         def run_deferred(n):
             for i in range(n):
-                if cursor[0] < len(deferred):
-                    deferred[cursor[0]]()
-                    cursor[0] = cursor[0] + 1
+                if done[0] < len(deferred):
+                    deferred[done[0]]()
+                    done[0] = done[0] + 1
 
-        def store_heads(dram, b, idx, o):
-            nc.sync.dma_start(
-                out=dram[b, idx * 4:(idx + 1) * 4, :, :].rearrange("h s d -> s h d"),
-                in_=o.rearrange("p (h d) -> p h d", h=4),
-            )
+        def store_block(dram, idx, o):
+            for b in range(B):
+                nc.sync.dma_start(
+                    out=dram[b, idx * HEADS:(idx + 1) * HEADS, :, :].rearrange("h (j e) d -> j h (e d)", e=RUN),
+                    in_=o[b:P:B, :].rearrange("p (h f) -> p h f", h=HEADS),
+                )
 
-        def store_batches(dram, h, o):
-            nc.sync.dma_start(
-                out=dram[:, h, :, :].rearrange("b s d -> s b d"),
-                in_=o.rearrange("p (b d) -> p b d", b=4),
-            )
+        block_out = {}
 
-        held = {}
-
-        def evacuate_key(i, acc, bias, store_it):
-            if i == 0:
-                held["pb"] = keyp.tile([P, 1024], F32, name="pb", tag="pb", bufs=4)
-                held["stores"] = []
-            pb = held["pb"]
-            stores = held["stores"]
-            stores.append(store_it)
-            nc.vector.tensor_tensor(
-                out=pb[:, i * 512:(i + 1) * 512].rearrange("p (a d) -> p a d", a=4),
-                in0=acc[:].rearrange("p (a d) -> p a d", a=4), in1=bias, op=ADD,
-            )
-            if i == 0:
-                return
-            pbv = pb[:].rearrange("p (a d) -> p a d", a=8)
-            mine = {}
-
-            def mul_cos():
-                mine["o"] = keyp.tile([P, 1024], F32, name="ko", tag="ko", bufs=4)
+        def evacuate(c, e, acc):
+            is_key, idx = BLOCKS[c]
+            cols = slice(idx * BLOCK, (idx + 1) * BLOCK)
+            if e == 0:
+                block_out[c] = outp.tile([P, RUN * BLOCK], F32, name="o", tag="o")
+            o = block_out[c]
+            ov = o[:].rearrange("p (h e d) -> p h e d", h=HEADS, e=RUN)[:, :, e, :]
+            accv = acc[:].rearrange("p (h d) -> p h d", h=HEADS)
+            if not is_key:
                 nc.vector.tensor_tensor(
-                    out=mine["o"][:].rearrange("p (a d) -> p a d", a=8), in0=pbv, in1=cos_b, op=MULT
+                    out=ov, in0=accv, in1=bias_v[:, cols].rearrange("p (h d) -> p h d", h=HEADS), op=ADD
                 )
+                if e == RUN - 1:
+                    store_block(out_1, idx, o)
+                return
+            pb = tmpp.tile([P, BLOCK], F32, name="pb", tag="pb")
+            nc.vector.tensor_tensor(out=pb[:], in0=acc[:], in1=bias_k[:, cols], op=ADD)
+            pbv = pb[:].rearrange("p (h d) -> p h d", h=HEADS)
+            held = {}
 
-            def mul_sin_lo():
-                mine["x"] = keyp.tile([P, 1024], F32, name="kx", tag="kx", bufs=2)
-                xv = mine["x"][:].rearrange("p (a d) -> p a d", a=8)
-                nc.vector.tensor_tensor(out=xv[:, :, 0:64], in0=pbv[:, :, 64:128], in1=sin_lo, op=MULT)
+            def times_cos():
+                nc.vector.tensor_tensor(out=ov, in0=pbv, in1=table(cosf, e, 0, HD), op=MULT)
 
-            def mul_sin_hi():
-                xv = mine["x"][:].rearrange("p (a d) -> p a d", a=8)
-                nc.vector.tensor_tensor(out=xv[:, :, 64:128], in0=pbv[:, :, 0:64], in1=sin_hi, op=MULT)
+            def times_sin():
+                t2 = tmpp.tile([P, BLOCK], F32, name="t2", tag="t2")
+                t2v = t2[:].rearrange("p (h d) -> p h d", h=HEADS)
+                nc.vector.tensor_tensor(out=t2v[:, :, 0:HALF], in0=pbv[:, :, HALF:HD], in1=table(sinf, e, 0, HALF), op=MULT)
+                nc.vector.tensor_tensor(out=t2v[:, :, HALF:HD], in0=pbv[:, :, 0:HALF], in1=table(sinf, e, HALF, HD), op=MULT)
+                held["t2"] = t2v
 
-            def combine():
-                o = mine["o"]
-                nc.vector.tensor_tensor(out=o[:], in0=o[:], in1=mine["x"][:], op=ADD)
-                stores[0](o[:, 0:512])
-                stores[1](o[:, 512:1024])
+            def add_and_store():
+                nc.vector.tensor_tensor(out=ov, in0=ov, in1=held["t2"], op=ADD)
+                if e == RUN - 1:
+                    store_block(out_0, idx, o)
 
-            deferred.extend([mul_cos, mul_sin_lo, mul_sin_hi, combine])
+            deferred.extend([times_cos, times_sin, add_and_store])
 
-        def evacuate(c, b, acc):
-            is_key, idx = CHUNKS[c]
-            cols = slice(idx * 512, (idx + 1) * 512)
-            if is_key:
-                evacuate_key(
-                    b % 2, acc, bias_k[:, cols].rearrange("p (a d) -> p a d", a=4),
-                    lambda o: store_heads(out_0, b, idx, o),
-                )
-            else:
-                o = outp.tile([P, 512], F32, name="o", tag="o")
-                nc.vector.tensor_tensor(out=o[:], in0=acc[:], in1=bias_v[:, cols], op=ADD)
-                store_heads(out_1, b, idx, o[:])
+        bias_targets = [bias_k[:, r * BLOCK:(r + 1) * BLOCK] for r in range(BIAS_ROWS)]
+        bias_targets.extend([bias_v[:, r * BLOCK:(r + 1) * BLOCK] for r in range(BIAS_ROWS)])
 
-        def evacuate_first(f, acc):
-            evacuate_key(
-                f % 2, acc, bias_k[:, f * HD:(f + 1) * HD].unsqueeze(1).to_broadcast([P, 4, HD]),
-                lambda o: store_batches(out_0, f, o),
-            )
+        def two_biases(first_row):
+            for row in range(first_row, first_row + 2):
+                broadcast_bias(row, bias_targets[row])
 
+        for first_row in range(0, 2 * BIAS_ROWS, 2):
+            two_biases(first_row)
         gx = {}
-        gx[0] = rows_to_grouped(raws["x"], 0)
-        gx[1] = rows_to_grouped(raws["x"], 1)
-        quantise(gx[0], xc, xs, 0)
-        for r in range(2):
-            broadcast_bias(r, bias_k[:, r * 512:(r + 1) * 512], False)
-        gx[2] = rows_to_grouped(raws["x"], 2)
-        quantise(gx[1], xc, xs, 1)
-        for r in range(2, 4):
-            broadcast_bias(r, bias_k[:, r * 512:(r + 1) * 512], False)
-        gx[3] = rows_to_grouped(raws["x"], 3)
-        quantise(gx[2], xc, xs, 2)
-        for r in range(2):
-            broadcast_bias(4 + r, bias_v[:, r * 512:(r + 1) * 512], False)
+        gx[0] = rows_to_grouped(raw_words["x"], 0, True)
+        for b in range(1, B):
+            gx[b] = rows_to_grouped(raw_words["x"], b, True)
+            quantise(gx[b - 1], xc, xs, b - 1)
 
-        new_wq(0)
-        wc0, ws0 = wq[0]
+        new_quantised(0)
+        wc0, ws0 = quantised[0]
         gw0 = {}
         acc0 = {}
 
-        def mx_first(f):
-            acc0[f] = accp.tile([P, 512], F32, name="acc", tag="acc")
+        def multiply_first(t):
             for b in range(B):
-                mx(acc0[f][:, b * P:(b + 1) * P], 0, b, lambda g: f * 512 + g * P, P)
+                if t == 0:
+                    acc0[b] = accp.tile([P, BANK], F32, name="acc", tag="acc")
+                multiply(acc0[b][:, t * P:(t + 1) * P], 0, b, lambda g: t * QWORDS + g * P, P)
 
-        gw0[0] = rows_to_grouped(raws[0], 0)
-        quantise(gx[3], xc, xs, 3)
-        for r in range(2, 4):
-            broadcast_bias(4 + r, bias_v[:, r * 512:(r + 1) * 512], False)
-        gw0[1] = rows_to_grouped(raws[0], 1)
+        gw0[0] = rows_to_grouped(raw_words[0], 0)
+        quantise(gx[B - 1], xc, xs, B - 1)
+        gw0[1] = rows_to_grouped(raw_words[0], 1)
         quantise(gw0[0], wc0, ws0, 0)
-        gw0[2] = rows_to_grouped(raws[0], 2)
+        gw0[2] = rows_to_grouped(raw_words[0], 2)
         quantise(gw0[1], wc0, ws0, 1)
-        mx_first(0)
-        gw0[3] = rows_to_grouped(raws[0], 3)
+        multiply_first(0)
+        gw0[3] = rows_to_grouped(raw_words[0], 3)
         quantise(gw0[2], wc0, ws0, 2)
-        evacuate_first(0, acc0[0])
-        mx_first(1)
-        evacuate_first(1, acc0[1])
-        mx_first(2)
-        new_wq(1)
-        wc1, ws1 = wq[1]
-        g10 = pass_to_grouped(raws[1], 0)
-        g11 = pass_to_grouped(raws[1], 1)
+        multiply_first(1)
+        multiply_first(2)
+        new_quantised(1)
+        wc1, ws1 = quantised[1]
+        gw1 = {}
+        gw1[0] = pass_to_grouped(raw_words[1], 0)
+        gw1[1] = pass_to_grouped(raw_words[1], 1)
         quantise(gw0[3], wc0, ws0, 3)
+        make_tables()
+        multiply_first(3)
+        quantise(gw1[0], wc1, ws1, 0)
+        evacuate(0, 0, acc0[0])
+        quantise(gw1[1], wc1, ws1, 1)
+        evacuate(0, 1, acc0[1])
+        gw1[2] = pass_to_grouped(raw_words[1], 2)
+        gw1[3] = pass_to_grouped(raw_words[1], 3)
+        evacuate(0, 2, acc0[2])
+        evacuate(0, 3, acc0[3])
+        load_weights(LOADS_AHEAD, 2)
         run_deferred(1)
-        evacuate_first(2, acc0[2])
-        mx_first(3)
-        quantise(g10, wc1, ws1, 0)
+        quantise(gw1[2], wc1, ws1, 2)
         run_deferred(1)
-        evacuate_first(3, acc0[3])
-        quantise(g11, wc1, ws1, 1)
-        g12 = pass_to_grouped(raws[1], 2)
-        g13 = pass_to_grouped(raws[1], 3)
-        run_deferred(1)
-        quantise(g12, wc1, ws1, 2)
-        run_deferred(1)
-        quantise(g13, wc1, ws1, 3)
-        load_w(4, 2)
+        quantise(gw1[3], wc1, ws1, 3)
 
         for c in range(1, LAST + 1):
             more = c < LAST
             for half in range(2):
                 if more:
                     if half == 0:
-                        new_wq(c + 1)
-                    wcn, wsn = wq[c + 1]
-                    ga = pass_to_grouped(raws[c + 1], 2 * half)
-                    gb = pass_to_grouped(raws[c + 1], 2 * half + 1)
-                run_deferred(1 if more else 2)
+                        new_quantised(c + 1)
+                    wcn, wsn = quantised[c + 1]
+                    ga = pass_to_grouped(raw_words[c + 1], 2 * half)
+                    gb = pass_to_grouped(raw_words[c + 1], 2 * half + 1)
+                run_deferred(DEFERRED_BEFORE_QUANTISE if more else 3)
                 if more:
                     quantise(ga, wcn, wsn, 2 * half)
-                acc_a = mx_group(c, 2 * half)
-                acc_b = mx_group(c, 2 * half + 1)
+                acc_a = multiply_block(c, 2 * half)
+                acc_b = multiply_block(c, 2 * half + 1)
+                run_deferred(DEFERRED_AFTER_MATMULS if more else 3)
                 evacuate(c, 2 * half, acc_a)
-                run_deferred(1 if more else 2)
                 if more:
                     quantise(gb, wcn, wsn, 2 * half + 1)
                 evacuate(c, 2 * half + 1, acc_b)
-            if c + 4 <= LAST:
-                load_w(c + 4, 2)
+            if c + LOADS_AHEAD <= LAST:
+                load_weights(c + LOADS_AHEAD, 2)
         run_deferred(len(deferred))

from contextlib import ExitStack

import concourse.mybir as mybir
from concourse.masks import make_identity

F32 = mybir.dt.float32
BF16 = mybir.dt.bfloat16
U32 = mybir.dt.uint32
U8 = mybir.dt.uint8
I32 = mybir.dt.int32
FP8X4 = mybir.dt.float8_e4m3fn_x4
ADD = mybir.AluOpType.add
MULT = mybir.AluOpType.mult

P = 128
B, S, DIM, H, HD = 4, 128, 2048, 16, 128
HALF = HD // 2
PASSES = DIM // (4 * P)
WORDS = DIM // 2
PASS_WORDS = WORDS // PASSES
BANK = 512
BLOCK = BANK
TILES = BLOCK // P
HEADS = BLOCK // HD
BIAS_ROWS = H * HD // BLOCK
RUN = 4
QWORDS = DIM // 4
FLOPS = 2 * B * S * DIM * 2 * H * HD

BLOCKS = [(True, 0), (False, 0), (True, 1), (False, 1), (True, 2), (False, 2), (True, 3), (False, 3)]
LAST = len(BLOCKS) - 1
LOADS_AHEAD = 4
DEFERRED_BEFORE_QUANTISE = 2
DEFERRED_AFTER_MATMULS = 1


def tile_attention_pb_kernel(tc, key_value, wk, bk, wv, bv, cos, sin, out_0, out_1):
    nc = tc.nc
    with ExitStack() as ctx:
        const = ctx.enter_context(tc.tile_pool(name="const", bufs=1))
        rawp = ctx.enter_context(tc.tile_pool(name="rawp", bufs=LOADS_AHEAD + 2))
        grp = ctx.enter_context(tc.tile_pool(name="grp", bufs=6))
        wqp = ctx.enter_context(tc.tile_pool(name="wqp", bufs=2))
        outp = ctx.enter_context(tc.tile_pool(name="outp", bufs=4))
        tmpp = ctx.enter_context(tc.tile_pool(name="tmpp", bufs=4))
        tps = ctx.enter_context(tc.psum_pool(name="tps", bufs=4))
        accp = ctx.enter_context(tc.psum_pool(name="accp", bufs=4))
        ctx.enter_context(tc.manual_schedule())

        raw_words = {}

        def load_activations():
            raw = rawp.tile([P, B * DIM], BF16, name="raw", tag="raw")
            for b in range(B):
                nc.sync.dma_start(out=raw[b:P:B, :], in_=key_value[b].rearrange("(j e) k -> j (e k)", e=RUN))
            raw_words["x"] = raw[:].bitcast(F32)

        def load_weights(c, pieces):
            is_key, idx = BLOCKS[c]
            w = wk if is_key else wv
            raw = rawp.tile([P, TILES * DIM], BF16, name="raw", tag="raw")
            per = TILES // pieces
            for i in range(pieces):
                rows = w[idx * BLOCK + i * per * P: idx * BLOCK + (i + 1) * per * P, :]
                nc.sync.dma_start(
                    out=raw[:, i * per * DIM:(i + 1) * per * DIM].rearrange("p (t k) -> p t k", t=per),
                    in_=rows.rearrange("(t p) k -> p t k", p=P),
                )
            raw_words[c] = raw[:].bitcast(F32)

        ident = const.tile([P, P], F32, name="ident")
        make_identity(nc, ident[:])
        identb = const.tile([P, P], BF16, name="identb")
        brows = const.tile([P, BLOCK], BF16, name="brows")
        cos_in = const.tile([P, RUN * HD], BF16, name="cos_in")
        sin_in = const.tile([P, RUN * HD], BF16, name="sin_in")
        cosf = const.tile([P, RUN * HD], F32, name="cosf")
        sinf = const.tile([P, RUN * HD], F32, name="sinf")
        bias_k = const.tile([P, H * HD], F32, name="bias_k")
        bias_v = const.tile([P, H * HD], F32, name="bias_v")
        xc = const.tile([P, B * QWORDS], U32, name="xc", align_bytes=64)
        xs = const.tile([P, B * QWORDS], U8, name="xs", align_bytes=64)

        nc.vector.memset(brows[:].bitcast(I32), 0)
        nc.scalar.dma_start(out=brows[0:BIAS_ROWS, :], in_=bk.rearrange("(r c) -> r c", c=BLOCK))
        nc.scalar.dma_start(out=brows[BIAS_ROWS:2 * BIAS_ROWS, :], in_=bv.rearrange("(r c) -> r c", c=BLOCK))
        for b in range(B):
            nc.gpsimd.dma_start(out=cos_in[b:P:B, :], in_=cos.rearrange("a b (j e) d -> (a b j) (e d)", e=RUN))
            nc.gpsimd.dma_start(out=sin_in[b:P:B, :], in_=sin.rearrange("a b (j e) d -> (a b j) (e d)", e=RUN))
        load_activations()
        load_weights(0, TILES)
        for c in range(1, LOADS_AHEAD):
            load_weights(c, 2)
        nc.vector.tensor_copy(out=identb[:], in_=ident[:])

        def make_tables():
            sin_v = sin_in[:].rearrange("p (e d) -> p e d", e=RUN)
            sinf_v = sinf[:].rearrange("p (e d) -> p e d", e=RUN)
            nc.vector.tensor_copy(out=cosf[:], in_=cos_in[:])
            nc.vector.tensor_scalar_mul(out=sinf_v[:, :, 0:HALF], in0=sin_v[:, :, 0:HALF], scalar1=-1.0)
            nc.vector.tensor_copy(out=sinf_v[:, :, HALF:HD], in_=sin_v[:, :, HALF:HD])

        def table(t, e, lo, hi):
            return t[:, e * HD + lo:e * HD + hi].unsqueeze(1).to_broadcast([P, HEADS, hi - lo])

        def broadcast_bias(row, dst):
            bank = accp.tile([P, BANK], F32, name="acc", tag="acc")
            nc.tensor.matmul(
                out=bank[:], lhsT=identb[:, row:row + 1].to_broadcast([P, P]), rhs=brows[:],
                start=True, stop=True,
            )
            nc.vector.tensor_copy(out=dst, in_=bank[:])

        def transpose_bank(words, cols):
            bank = tps.tile([P, BANK], F32, name="tbank", tag="tbank")
            for j in range(4):
                nc.tensor.transpose(
                    out=bank[:, j * P:(j + 1) * P], in_=words[:, cols[j]:cols[j] + P], identity=ident[:]
                )
            return bank

        def rows_to_grouped(words, t, share=False):
            banks = [transpose_bank(words, [t * WORDS + (4 * gp + j) * P for j in range(4)]) for gp in range(2)]
            grouped = grp.tile([P, DIM], BF16, name="grouped", tag="grouped", align_bytes=64)
            gw = grouped[:].bitcast(F32)
            for gp in range(2):
                copy = nc.vector.tensor_copy if (share and gp == 1) else nc.scalar.copy
                copy(
                    out=gw[:, gp * BANK:(gp + 1) * BANK].rearrange("p (g r u) -> p g r u", g=2, u=2),
                    in_=banks[gp][:].rearrange("p (g u r) -> p g r u", g=2, u=2),
                )
            return grouped

        def pass_to_grouped(words, g):
            banks = [
                transpose_bank(words, [(2 * fp + (j % 2)) * WORDS + PASS_WORDS * g + P * (j // 2) for j in range(4)])
                for fp in range(2)
            ]
            grouped = grp.tile([P, DIM], BF16, name="grouped", tag="grouped", align_bytes=64)
            gw = grouped[:].bitcast(F32)
            for fp in range(2):
                nc.scalar.copy(
                    out=gw[:, fp * BANK:(fp + 1) * BANK].rearrange("p (f u) -> p f u", u=2),
                    in_=banks[fp][:].rearrange("p (u f) -> p f u", u=2),
                )
            return grouped

        def quantise(grouped, codes, scales, part):
            cols = slice(part * QWORDS, (part + 1) * QWORDS)
            nc.vector.quantize_mx(out=codes[:, cols].bitcast(FP8X4), scales=scales[:, cols], in_=grouped[:])

        quantised = {}

        def new_quantised(c):
            wc = wqp.tile([P, PASSES * QWORDS], U32, name="wc", tag="wc", align_bytes=64)
            ws = wqp.tile([P, PASSES * QWORDS], U8, name="ws", tag="ws", align_bytes=64)
            quantised[c] = (wc, ws)

        def multiply(acc_cols, c, b, first_col, n):
            wc, ws = quantised[c]
            for g in range(PASSES):
                xcols = slice(b * QWORDS + g * P, b * QWORDS + (g + 1) * P)
                wcols = slice(first_col(g), first_col(g) + n)
                nc.tensor.matmul_mx(
                    out=acc_cols,
                    lhsT=xc[:, xcols].bitcast(FP8X4), lhsT_scale=xs[:, xcols],
                    rhs=wc[:, wcols].bitcast(FP8X4), rhs_scale=ws[:, wcols],
                    start=(g == 0), stop=(g == PASSES - 1),
                )

        def multiply_block(c, b):
            acc = accp.tile([P, BANK], F32, name="acc", tag="acc")
            multiply(acc[:], c, b, lambda g: g * QWORDS, BLOCK)
            return acc

        deferred = []
        done = [0]

        def run_deferred(n):
            for i in range(n):
                if done[0] < len(deferred):
                    deferred[done[0]]()
                    done[0] = done[0] + 1

        def store_block(dram, idx, o):
            for b in range(B):
                nc.sync.dma_start(
                    out=dram[b, idx * HEADS:(idx + 1) * HEADS, :, :].rearrange("h (j e) d -> j h (e d)", e=RUN),
                    in_=o[b:P:B, :].rearrange("p (h f) -> p h f", h=HEADS),
                )

        block_out = {}

        def evacuate(c, e, acc):
            is_key, idx = BLOCKS[c]
            cols = slice(idx * BLOCK, (idx + 1) * BLOCK)
            if e == 0:
                block_out[c] = outp.tile([P, RUN * BLOCK], F32, name="o", tag="o")
            o = block_out[c]
            ov = o[:].rearrange("p (h e d) -> p h e d", h=HEADS, e=RUN)[:, :, e, :]
            accv = acc[:].rearrange("p (h d) -> p h d", h=HEADS)
            if not is_key:
                nc.vector.tensor_tensor(
                    out=ov, in0=accv, in1=bias_v[:, cols].rearrange("p (h d) -> p h d", h=HEADS), op=ADD
                )
                if e == RUN - 1:
                    store_block(out_1, idx, o)
                return
            pb = tmpp.tile([P, BLOCK], F32, name="pb", tag="pb")
            nc.vector.tensor_tensor(out=pb[:], in0=acc[:], in1=bias_k[:, cols], op=ADD)
            pbv = pb[:].rearrange("p (h d) -> p h d", h=HEADS)
            held = {}

            def times_cos():
                nc.vector.tensor_tensor(out=ov, in0=pbv, in1=table(cosf, e, 0, HD), op=MULT)

            def times_sin():
                t2 = tmpp.tile([P, BLOCK], F32, name="t2", tag="t2")
                t2v = t2[:].rearrange("p (h d) -> p h d", h=HEADS)
                nc.vector.tensor_tensor(out=t2v[:, :, 0:HALF], in0=pbv[:, :, HALF:HD], in1=table(sinf, e, 0, HALF), op=MULT)
                nc.vector.tensor_tensor(out=t2v[:, :, HALF:HD], in0=pbv[:, :, 0:HALF], in1=table(sinf, e, HALF, HD), op=MULT)
                held["t2"] = t2v

            def add_and_store():
                nc.vector.tensor_tensor(out=ov, in0=ov, in1=held["t2"], op=ADD)
                if e == RUN - 1:
                    store_block(out_0, idx, o)

            deferred.extend([times_cos, times_sin, add_and_store])

        bias_targets = [bias_k[:, r * BLOCK:(r + 1) * BLOCK] for r in range(BIAS_ROWS)]
        bias_targets.extend([bias_v[:, r * BLOCK:(r + 1) * BLOCK] for r in range(BIAS_ROWS)])

        def two_biases(first_row):
            for row in range(first_row, first_row + 2):
                broadcast_bias(row, bias_targets[row])

        for first_row in range(0, 2 * BIAS_ROWS, 2):
            two_biases(first_row)
        gx = {}
        gx[0] = rows_to_grouped(raw_words["x"], 0, True)
        for b in range(1, B):
            gx[b] = rows_to_grouped(raw_words["x"], b, True)
            quantise(gx[b - 1], xc, xs, b - 1)

        new_quantised(0)
        wc0, ws0 = quantised[0]
        gw0 = {}
        acc0 = {}

        def multiply_first(t):
            for b in range(B):
                if t == 0:
                    acc0[b] = accp.tile([P, BANK], F32, name="acc", tag="acc")
                multiply(acc0[b][:, t * P:(t + 1) * P], 0, b, lambda g: t * QWORDS + g * P, P)

        gw0[0] = rows_to_grouped(raw_words[0], 0)
        quantise(gx[B - 1], xc, xs, B - 1)
        gw0[1] = rows_to_grouped(raw_words[0], 1)
        quantise(gw0[0], wc0, ws0, 0)
        gw0[2] = rows_to_grouped(raw_words[0], 2)
        quantise(gw0[1], wc0, ws0, 1)
        multiply_first(0)
        gw0[3] = rows_to_grouped(raw_words[0], 3)
        quantise(gw0[2], wc0, ws0, 2)
        multiply_first(1)
        multiply_first(2)
        new_quantised(1)
        wc1, ws1 = quantised[1]
        gw1 = {}
        gw1[0] = pass_to_grouped(raw_words[1], 0)
        gw1[1] = pass_to_grouped(raw_words[1], 1)
        quantise(gw0[3], wc0, ws0, 3)
        make_tables()
        multiply_first(3)
        quantise(gw1[0], wc1, ws1, 0)
        evacuate(0, 0, acc0[0])
        quantise(gw1[1], wc1, ws1, 1)
        evacuate(0, 1, acc0[1])
        gw1[2] = pass_to_grouped(raw_words[1], 2)
        gw1[3] = pass_to_grouped(raw_words[1], 3)
        evacuate(0, 2, acc0[2])
        evacuate(0, 3, acc0[3])
        load_weights(LOADS_AHEAD, 2)
        run_deferred(1)
        quantise(gw1[2], wc1, ws1, 2)
        run_deferred(1)
        quantise(gw1[3], wc1, ws1, 3)

        for c in range(1, LAST + 1):
            more = c < LAST
            for half in range(2):
                if more:
                    if half == 0:
                        new_quantised(c + 1)
                    wcn, wsn = quantised[c + 1]
                    ga = pass_to_grouped(raw_words[c + 1], 2 * half)
                    gb = pass_to_grouped(raw_words[c + 1], 2 * half + 1)
                run_deferred(DEFERRED_BEFORE_QUANTISE if more else 3)
                if more:
                    quantise(ga, wcn, wsn, 2 * half)
                acc_a = multiply_block(c, 2 * half)
                acc_b = multiply_block(c, 2 * half + 1)
                run_deferred(DEFERRED_AFTER_MATMULS if more else 3)
                evacuate(c, 2 * half, acc_a)
                if more:
                    quantise(gb, wcn, wsn, 2 * half + 1)
                evacuate(c, 2 * half + 1, acc_b)
            if c + LOADS_AHEAD <= LAST:
                load_weights(c + LOADS_AHEAD, 2)
        run_deferred(len(deferred))
